import numpy as np
import ml_dtypes


def mxq(x, axis, fmt="e4m3"):
    dtype, down = {"e4m3": (ml_dtypes.float8_e4m3fn, 7), "e5m2": (ml_dtypes.float8_e5m2, 14)}[fmt]
    v = np.moveaxis(np.asarray(x, np.float32).astype(ml_dtypes.bfloat16).astype(np.float64), axis, -1)
    blocks = v.reshape(v.shape[:-1] + (-1, 32))
    amax = np.abs(blocks).max(-1, keepdims=True)
    byte = np.maximum(np.where(amax > 0, np.frexp(amax)[1] - 1 + 127, 0) - down, 1)
    scale = np.exp2(byte - 127.0)
    codes = (blocks / scale).astype(np.float32).astype(dtype).astype(np.float64)
    return np.moveaxis((codes * scale).reshape(v.shape), -1, axis)


WIDE = False


def mx_kscale(k):
    if not WIDE:
        return np.ones(k)
    levels = np.array([10, -10, 5, -5, 0])
    a = np.random.permutation(np.resize(levels, k // 512 * 4)).reshape(k // 512, 4)
    idx = np.arange(k)
    return np.exp2(a[idx // 512, idx % 128 // 32])


BF16 = ml_dtypes.bfloat16


def bf(x):
    return np.asarray(x, np.float32).astype(BF16)


def f64(x):
    return np.asarray(x).astype(np.float64)


B, S, H, HD = 1, 512, 4, 128
D = H * HD


def silu(x):
    e = np.exp(-np.abs(x))
    return x * np.where(x >= 0.0, 1.0, e) / (1.0 + e)


def split_heads(x):
    return x.reshape(B, S, H, HD).transpose(0, 2, 1, 3)


def setup_inputs():
    s = mx_kscale(S)
    c = (s / s.min())[None, :, None]
    return {"v": bf(np.random.standard_normal((B, S, D)) * 4.0 / np.sqrt(S) / c),
            "k": bf(np.random.standard_normal((B, S, D)) * 1.2 / HD ** 0.25 * c),
            "q": bf(np.random.standard_normal((B, S, D)) * 1.2 / HD ** 0.25)}


def reference(v, k, q):
    qh = split_heads(f64(q))
    kh = split_heads(f64(k))
    vh = split_heads(f64(v))
    scores = qh @ kh.transpose(0, 1, 3, 2)
    p = silu(scores)
    av = mxq(p, 3, "e4m3") @ mxq(vh, 2, "e4m3")
    return av.transpose(0, 2, 1, 3).reshape(B, S, D)

@@ -1,0 +1,149 @@
+from contextlib import ExitStack
+
+import concourse.mybir as mybir
+from concourse.masks import make_identity
+
+BF16 = mybir.dt.bfloat16
+F32 = mybir.dt.float32
+U32 = mybir.dt.uint32
+U8 = mybir.dt.uint8
+FP8X4 = mybir.dt.float8_e4m3fn_x4
+SILU = mybir.ActivationFunctionType.Silu
+
+P = 128
+PACK = 4
+S = 512
+H = 4
+HD = 128
+SLOTS = S // P
+UNITS = H * SLOTS
+
+SCORES_AHEAD = 2
+MX_BEHIND = 2
+
+FLOPS = 2 * (2 * H * S * S * HD)
+
+
+def tile_pointwisespaggregatedattention_s_kernel(tc, v, k, q, out):
+    nc = tc.nc
+    assert SLOTS == PACK
+
+    def by_partition(x):
+        return x.flatten_outer_dims().rearrange("(p j) d -> p j d", j=SLOTS)
+
+    v_rows, k_rows, q_rows, out_rows = by_partition(v), by_partition(k), by_partition(q), by_partition(out)
+
+    with ExitStack() as ctx:
+        consts = ctx.enter_context(tc.tile_pool(name="consts", bufs=1))
+        loads = ctx.enter_context(tc.tile_pool(name="loads", bufs=H))
+        heads = ctx.enter_context(tc.tile_pool(name="heads", bufs=2))
+        units = ctx.enter_context(tc.tile_pool(name="units", bufs=SCORES_AHEAD + MX_BEHIND))
+        flipped_psum = ctx.enter_context(tc.psum_pool(name="flipped_psum", bufs=2))
+        scores_psum = ctx.enter_context(tc.psum_pool(name="scores_psum", bufs=4))
+        out_psum = ctx.enter_context(tc.psum_pool(name="out_psum", bufs=2))
+
+        k_sb, q_sb, v_sb = {}, {}, {}
+        kT, qT = {}, {}
+        v_codes, v_scales = {}, {}
+        scores, p_codes, p_scales = {}, {}, {}
+
+        def load(h):
+            cols = slice(h * HD, (h + 1) * HD)
+            k_h = loads.tile([P, SLOTS, HD], BF16)
+            nc.sync.dma_start(out=k_h[:], in_=k_rows[:, :, cols])
+            q_h = loads.tile([P, SLOTS, HD], BF16)
+            nc.sync.dma_start(out=q_h[:], in_=q_rows[:, :, cols])
+            v_h = loads.tile([P, SLOTS, HD], BF16)
+            nc.sync.dma_start(out=v_h[:], in_=v_rows[:, :, cols])
+            k_sb[h], q_sb[h], v_sb[h] = k_h, q_h, v_h
+
+        def flip(x_h):
+            flipped = flipped_psum.tile([P, SLOTS, P], BF16)
+            for j in range(SLOTS):
+                nc.tensor.transpose(flipped[:, j, :], x_h[:, j, :], identity[:])
+            xT_h = heads.tile([P, SLOTS, P], BF16, tag="xT", bufs=4)
+            nc.vector.tensor_copy(out=xT_h[:], in_=flipped[:])
+            return xT_h
+
+        def quantise_v(h):
+            grouped = heads.tile([P, HD, PACK], BF16, align_bytes=64)
+            nc.vector.tensor_copy(out=grouped[:], in_=v_sb[h][:].rearrange("p j d -> p d j"))
+            codes = heads.tile([P, HD], U32, align_bytes=64)
+            planes = heads.tile([P, HD], U8, align_bytes=64)
+            nc.vector.quantize_mx(
+                out=codes[:].bitcast(FP8X4),
+                scales=planes[:],
+                in_=grouped[:].rearrange("p d j -> p (d j)"),
+            )
+            v_codes[h], v_scales[h] = codes, planes
+
+        def write_scores(u):
+            h, slot = divmod(u, SLOTS)
+            bank = scores_psum.tile([P, PACK, P], F32)
+            for j in range(PACK):
+                nc.tensor.matmul(
+                    out=bank[:, j, :], lhsT=kT[h][:, j, :], rhs=qT[h][:, slot, :], start=True, stop=True
+                )
+            scores[u] = bank
+
+        def silu_and_quantise(u):
+            grouped = units.tile([P, P, PACK], BF16, align_bytes=64)
+            nc.scalar.activation(out=grouped[:], in_=scores[u][:].rearrange("p j n -> p n j"), func=SILU)
+            codes = units.tile([P, P], U32, align_bytes=64)
+            planes = units.tile([P, P], U8, align_bytes=64)
+            nc.vector.quantize_mx(
+                out=codes[:].bitcast(FP8X4),
+                scales=planes[:],
+                in_=grouped[:].rearrange("p n j -> p (n j)"),
+            )
+            p_codes[u], p_scales[u] = codes, planes
+
+        def multiply_by_v(u):
+            h, slot = divmod(u, SLOTS)
+            acc = out_psum.tile([P, HD], F32)
+            nc.tensor.matmul_mx(
+                out=acc[:],
+                lhsT=p_codes[u][:].bitcast(FP8X4),
+                lhsT_scale=p_scales[u][:],
+                rhs=v_codes[h][:].bitcast(FP8X4),
+                rhs_scale=v_scales[h][:],
+                start=True,
+                stop=True,
+            )
+            result = units.tile([P, HD], F32)
+            nc.vector.tensor_copy(out=result[:], in_=acc[:])
+            nc.sync.dma_start(out=out_rows[:, slot, h * HD : (h + 1) * HD], in_=result[:])
+
+        ctx.enter_context(tc.manual_schedule())
+
+        for h in range(H):
+            load(h)
+
+        identity = consts.tile([P, P], BF16)
+        make_identity(nc, identity[:])
+        zero = consts.tile([P, 1], F32)
+        nc.vector.memset(zero[:], 0.0)
+        warm = consts.tile([P, 1], F32)
+        nc.scalar.activation(out=warm[:], in_=zero[:], func=SILU)
+
+        kT[0] = flip(k_sb[0])
+        qT[0] = flip(q_sb[0])
+        for u in range(SCORES_AHEAD):
+            write_scores(u)
+        quantise_v(0)
+
+        for u in range(UNITS + MX_BEHIND):
+            h, slot = divmod(u, SLOTS)
+            if h + 1 < H:
+                if slot == 0:
+                    kT[h + 1] = flip(k_sb[h + 1])
+                if slot == 1:
+                    qT[h + 1] = flip(q_sb[h + 1])
+                if slot == 2:
+                    quantise_v(h + 1)
+            if u + SCORES_AHEAD < UNITS:
+                write_scores(u + SCORES_AHEAD)
+            if u < UNITS:
+                silu_and_quantise(u)
+            if u >= MX_BEHIND:
+                multiply_by_v(u - MX_BEHIND)

@@ -19,7 +19,7 @@ SLOTS = S // P
 UNITS = H * SLOTS
 
 SCORES_AHEAD = 2
-MX_BEHIND = 2
+MX_BEHIND = 3
 
 FLOPS = 2 * (2 * H * S * S * HD)
 
@@ -35,9 +35,8 @@ def tile_pointwisespaggregatedattention_s_kernel(tc, v, k, q, out):
 
     with ExitStack() as ctx:
         consts = ctx.enter_context(tc.tile_pool(name="consts", bufs=1))
-        loads = ctx.enter_context(tc.tile_pool(name="loads", bufs=H))
-        heads = ctx.enter_context(tc.tile_pool(name="heads", bufs=2))
-        units = ctx.enter_context(tc.tile_pool(name="units", bufs=SCORES_AHEAD + MX_BEHIND))
+        heads = ctx.enter_context(tc.tile_pool(name="heads", bufs=H))
+        units = ctx.enter_context(tc.tile_pool(name="units", bufs=SCORES_AHEAD + MX_BEHIND + 1))
         flipped_psum = ctx.enter_context(tc.psum_pool(name="flipped_psum", bufs=2))
         scores_psum = ctx.enter_context(tc.psum_pool(name="scores_psum", bufs=4))
         out_psum = ctx.enter_context(tc.psum_pool(name="out_psum", bufs=2))
@@ -46,22 +45,26 @@ def tile_pointwisespaggregatedattention_s_kernel(tc, v, k, q, out):
         kT, qT = {}, {}
         v_codes, v_scales = {}, {}
         scores, p_codes, p_scales = {}, {}, {}
+        out_sb = consts.tile([P, SLOTS, H * HD], F32)
 
         def load(h):
             cols = slice(h * HD, (h + 1) * HD)
-            k_h = loads.tile([P, SLOTS, HD], BF16)
+            k_h = heads.tile([P, SLOTS, HD], BF16)
             nc.sync.dma_start(out=k_h[:], in_=k_rows[:, :, cols])
-            q_h = loads.tile([P, SLOTS, HD], BF16)
+            q_h = heads.tile([P, SLOTS, HD], BF16)
             nc.sync.dma_start(out=q_h[:], in_=q_rows[:, :, cols])
-            v_h = loads.tile([P, SLOTS, HD], BF16)
+            v_h = heads.tile([P, SLOTS, HD], BF16)
             nc.sync.dma_start(out=v_h[:], in_=v_rows[:, :, cols])
             k_sb[h], q_sb[h], v_sb[h] = k_h, q_h, v_h
 
-        def flip(x_h):
+        def transpose_slots(x_h):
             flipped = flipped_psum.tile([P, SLOTS, P], BF16)
             for j in range(SLOTS):
                 nc.tensor.transpose(flipped[:, j, :], x_h[:, j, :], identity[:])
-            xT_h = heads.tile([P, SLOTS, P], BF16, tag="xT", bufs=4)
+            return flipped
+
+        def copy_out(flipped):
+            xT_h = heads.tile([P, SLOTS, P], BF16, tag="xT", bufs=2 * H)
             nc.vector.tensor_copy(out=xT_h[:], in_=flipped[:])
             return xT_h
 
@@ -100,6 +103,7 @@ def tile_pointwisespaggregatedattention_s_kernel(tc, v, k, q, out):
 
         def multiply_by_v(u):
             h, slot = divmod(u, SLOTS)
+            cols = slice(h * HD, (h + 1) * HD)
             acc = out_psum.tile([P, HD], F32)
             nc.tensor.matmul_mx(
                 out=acc[:],
@@ -110,9 +114,8 @@ def tile_pointwisespaggregatedattention_s_kernel(tc, v, k, q, out):
                 start=True,
                 stop=True,
             )
-            result = units.tile([P, HD], F32)
-            nc.vector.tensor_copy(out=result[:], in_=acc[:])
-            nc.sync.dma_start(out=out_rows[:, slot, h * HD : (h + 1) * HD], in_=result[:])
+            nc.vector.tensor_copy(out=out_sb[:, slot, cols], in_=acc[:])
+            nc.sync.dma_start(out=out_rows[:, slot, cols], in_=out_sb[:, slot, cols])
 
         ctx.enter_context(tc.manual_schedule())
 
@@ -126,24 +129,31 @@ def tile_pointwisespaggregatedattention_s_kernel(tc, v, k, q, out):
         warm = consts.tile([P, 1], F32)
         nc.scalar.activation(out=warm[:], in_=zero[:], func=SILU)
 
-        kT[0] = flip(k_sb[0])
-        qT[0] = flip(q_sb[0])
+        kT[0] = copy_out(transpose_slots(k_sb[0]))
+        qT[0] = copy_out(transpose_slots(q_sb[0]))
         for u in range(SCORES_AHEAD):
             write_scores(u)
         quantise_v(0)
 
-        for u in range(UNITS + MX_BEHIND):
+        for u in range(-SCORES_AHEAD, UNITS + MX_BEHIND):
+            ahead = u + SCORES_AHEAD
+            ahead_h, ahead_slot = divmod(ahead, SLOTS)
             h, slot = divmod(u, SLOTS)
-            if h + 1 < H:
-                if slot == 0:
-                    kT[h + 1] = flip(k_sb[h + 1])
-                if slot == 1:
-                    qT[h + 1] = flip(q_sb[h + 1])
-                if slot == 2:
-                    quantise_v(h + 1)
-            if u + SCORES_AHEAD < UNITS:
-                write_scores(u + SCORES_AHEAD)
-            if u < UNITS:
-                silu_and_quantise(u)
-            if u >= MX_BEHIND:
+
+            flipped = None
+            if ahead_h + 1 < H and ahead_slot == 0:
+                flipped = transpose_slots(k_sb[ahead_h + 1])
+            if ahead_h + 1 < H and ahead_slot == 1:
+                flipped = transpose_slots(q_sb[ahead_h + 1])
+            if SCORES_AHEAD <= ahead < UNITS:
+                write_scores(ahead)
+            if 0 <= u - MX_BEHIND:
                 multiply_by_v(u - MX_BEHIND)
+            if 0 <= u < UNITS:
+                silu_and_quantise(u)
+            if flipped is not None and ahead_slot == 0:
+                kT[ahead_h + 1] = copy_out(flipped)
+            if flipped is not None and ahead_slot == 1:
+                qT[ahead_h + 1] = copy_out(flipped)
+            if 0 <= h and h + 1 < H and slot == 1:
+                quantise_v(h + 1)

@@ -20,6 +20,7 @@ UNITS = H * SLOTS
 
 SCORES_AHEAD = 2
 MX_BEHIND = 3
+WARM_PASSES = 16
 
 FLOPS = 2 * (2 * H * S * S * HD)
 
@@ -104,7 +105,7 @@ def tile_pointwisespaggregatedattention_s_kernel(tc, v, k, q, out):
         def multiply_by_v(u):
             h, slot = divmod(u, SLOTS)
             cols = slice(h * HD, (h + 1) * HD)
-            acc = out_psum.tile([P, HD], F32)
+            acc = out_psum.tile([P, HD], F32, tag="acc")
             nc.tensor.matmul_mx(
                 out=acc[:],
                 lhsT=p_codes[u][:].bitcast(FP8X4),
@@ -128,6 +129,23 @@ def tile_pointwisespaggregatedattention_s_kernel(tc, v, k, q, out):
         nc.vector.memset(zero[:], 0.0)
         warm = consts.tile([P, 1], F32)
         nc.scalar.activation(out=warm[:], in_=zero[:], func=SILU)
+
+        zeros = consts.tile([P, PACK * P], BF16, align_bytes=64)
+        nc.vector.memset(zeros[:], 0.0)
+        zero_codes = consts.tile([P, P], U32, align_bytes=64)
+        zero_planes = consts.tile([P, P], U8, align_bytes=64)
+        nc.vector.quantize_mx(out=zero_codes[:].bitcast(FP8X4), scales=zero_planes[:], in_=zeros[:])
+        for i in range(WARM_PASSES):
+            unread = out_psum.tile([P, HD], F32, tag="acc")
+            nc.tensor.matmul_mx(
+                out=unread[:],
+                lhsT=zero_codes[:].bitcast(FP8X4),
+                lhsT_scale=zero_planes[:],
+                rhs=zero_codes[:].bitcast(FP8X4),
+                rhs_scale=zero_planes[:],
+                start=True,
+                stop=True,
+            )
 
         kT[0] = copy_out(transpose_slots(k_sb[0]))
         qT[0] = copy_out(transpose_slots(q_sb[0]))

@@ -16,11 +16,11 @@ S = 512
 H = 4
 HD = 128
 SLOTS = S // P
+PAIR = 2
 UNITS = H * SLOTS
 
 SCORES_AHEAD = 2
-MX_BEHIND = 3
-WARM_PASSES = 16
+MX_BEHIND = 4
 
 FLOPS = 2 * (2 * H * S * S * HD)
 
@@ -38,9 +38,8 @@ def tile_pointwisespaggregatedattention_s_kernel(tc, v, k, q, out):
         consts = ctx.enter_context(tc.tile_pool(name="consts", bufs=1))
         heads = ctx.enter_context(tc.tile_pool(name="heads", bufs=H))
         units = ctx.enter_context(tc.tile_pool(name="units", bufs=SCORES_AHEAD + MX_BEHIND + 1))
-        flipped_psum = ctx.enter_context(tc.psum_pool(name="flipped_psum", bufs=2))
         scores_psum = ctx.enter_context(tc.psum_pool(name="scores_psum", bufs=4))
-        out_psum = ctx.enter_context(tc.psum_pool(name="out_psum", bufs=2))
+        small_psum = ctx.enter_context(tc.psum_pool(name="small_psum", bufs=4))
 
         k_sb, q_sb, v_sb = {}, {}, {}
         kT, qT = {}, {}
@@ -48,25 +47,35 @@ def tile_pointwisespaggregatedattention_s_kernel(tc, v, k, q, out):
         scores, p_codes, p_scales = {}, {}, {}
         out_sb = consts.tile([P, SLOTS, H * HD], F32)
 
+        def load_in_pairs(x_rows, h):
+            x_h = heads.tile([P, SLOTS, HD], BF16, tag="x", bufs=2 * H)
+            for first in range(0, SLOTS, PAIR):
+                nc.sync.dma_start(
+                    out=x_h[:, first : first + PAIR, :],
+                    in_=x_rows[:, first : first + PAIR, h * HD : (h + 1) * HD],
+                )
+            return x_h
+
         def load(h):
-            cols = slice(h * HD, (h + 1) * HD)
-            k_h = heads.tile([P, SLOTS, HD], BF16)
-            nc.sync.dma_start(out=k_h[:], in_=k_rows[:, :, cols])
-            q_h = heads.tile([P, SLOTS, HD], BF16)
-            nc.sync.dma_start(out=q_h[:], in_=q_rows[:, :, cols])
+            k_sb[h] = load_in_pairs(k_rows, h)
+            q_sb[h] = load_in_pairs(q_rows, h)
             v_h = heads.tile([P, SLOTS, HD], BF16)
-            nc.sync.dma_start(out=v_h[:], in_=v_rows[:, :, cols])
-            k_sb[h], q_sb[h], v_sb[h] = k_h, q_h, v_h
+            nc.sync.dma_start(out=v_h[:], in_=v_rows[:, :, h * HD : (h + 1) * HD])
+            v_sb[h] = v_h
 
         def transpose_slots(x_h):
-            flipped = flipped_psum.tile([P, SLOTS, P], BF16)
-            for j in range(SLOTS):
-                nc.tensor.transpose(flipped[:, j, :], x_h[:, j, :], identity[:])
-            return flipped
+            banks = []
+            for first in range(0, SLOTS, PAIR):
+                flipped = small_psum.tile([P, PAIR, P], BF16, tag="small")
+                for j in range(PAIR):
+                    nc.tensor.transpose(flipped[:, j, :], x_h[:, first + j, :], identity[:])
+                banks.append(flipped)
+            return banks
 
-        def copy_out(flipped):
+        def copy_out(banks):
             xT_h = heads.tile([P, SLOTS, P], BF16, tag="xT", bufs=2 * H)
-            nc.vector.tensor_copy(out=xT_h[:], in_=flipped[:])
+            for i, flipped in enumerate(banks):
+                nc.vector.tensor_copy(out=xT_h[:, i * PAIR : (i + 1) * PAIR, :], in_=flipped[:])
             return xT_h
 
         def quantise_v(h):
@@ -105,7 +114,7 @@ def tile_pointwisespaggregatedattention_s_kernel(tc, v, k, q, out):
         def multiply_by_v(u):
             h, slot = divmod(u, SLOTS)
             cols = slice(h * HD, (h + 1) * HD)
-            acc = out_psum.tile([P, HD], F32, tag="acc")
+            acc = small_psum.tile([P, HD], F32, tag="small")
             nc.tensor.matmul_mx(
                 out=acc[:],
                 lhsT=p_codes[u][:].bitcast(FP8X4),
@@ -130,23 +139,6 @@ def tile_pointwisespaggregatedattention_s_kernel(tc, v, k, q, out):
         warm = consts.tile([P, 1], F32)
         nc.scalar.activation(out=warm[:], in_=zero[:], func=SILU)
 
-        zeros = consts.tile([P, PACK * P], BF16, align_bytes=64)
-        nc.vector.memset(zeros[:], 0.0)
-        zero_codes = consts.tile([P, P], U32, align_bytes=64)
-        zero_planes = consts.tile([P, P], U8, align_bytes=64)
-        nc.vector.quantize_mx(out=zero_codes[:].bitcast(FP8X4), scales=zero_planes[:], in_=zeros[:])
-        for i in range(WARM_PASSES):
-            unread = out_psum.tile([P, HD], F32, tag="acc")
-            nc.tensor.matmul_mx(
-                out=unread[:],
-                lhsT=zero_codes[:].bitcast(FP8X4),
-                lhsT_scale=zero_planes[:],
-                rhs=zero_codes[:].bitcast(FP8X4),
-                rhs_scale=zero_planes[:],
-                start=True,
-                stop=True,
-            )
-
         kT[0] = copy_out(transpose_slots(k_sb[0]))
         qT[0] = copy_out(transpose_slots(q_sb[0]))
         for u in range(SCORES_AHEAD):
@@ -158,20 +150,15 @@ def tile_pointwisespaggregatedattention_s_kernel(tc, v, k, q, out):
             ahead_h, ahead_slot = divmod(ahead, SLOTS)
             h, slot = divmod(u, SLOTS)
 
-            flipped = None
             if ahead_h + 1 < H and ahead_slot == 0:
-                flipped = transpose_slots(k_sb[ahead_h + 1])
+                kT[ahead_h + 1] = copy_out(transpose_slots(k_sb[ahead_h + 1]))
             if ahead_h + 1 < H and ahead_slot == 1:
-                flipped = transpose_slots(q_sb[ahead_h + 1])
+                qT[ahead_h + 1] = copy_out(transpose_slots(q_sb[ahead_h + 1]))
             if SCORES_AHEAD <= ahead < UNITS:
                 write_scores(ahead)
             if 0 <= u - MX_BEHIND:
                 multiply_by_v(u - MX_BEHIND)
             if 0 <= u < UNITS:
                 silu_and_quantise(u)
-            if flipped is not None and ahead_slot == 0:
-                kT[ahead_h + 1] = copy_out(flipped)
-            if flipped is not None and ahead_slot == 1:
-                qT[ahead_h + 1] = copy_out(flipped)
-            if 0 <= h and h + 1 < H and slot == 1:
+            if 0 <= h and h + 1 < H and slot == 2:
                 quantise_v(h + 1)

@@ -19,8 +19,8 @@ SLOTS = S // P
 PAIR = 2
 UNITS = H * SLOTS
 
-SCORES_AHEAD = 2
-MX_BEHIND = 4
+SCORES_AHEAD = 3
+MX_BEHIND = 2
 
 FLOPS = 2 * (2 * H * S * S * HD)
 
@@ -43,56 +43,46 @@ def tile_pointwisespaggregatedattention_s_kernel(tc, v, k, q, out):
 
         k_sb, q_sb, v_sb = {}, {}, {}
         kT, qT = {}, {}
-        v_codes, v_scales = {}, {}
+        v_grouped, v_codes, v_scales = {}, {}, {}
         scores, p_codes, p_scales = {}, {}, {}
+        results = {}
         out_sb = consts.tile([P, SLOTS, H * HD], F32)
 
-        def load_in_pairs(x_rows, h):
-            x_h = heads.tile([P, SLOTS, HD], BF16, tag="x", bufs=2 * H)
-            for first in range(0, SLOTS, PAIR):
-                nc.sync.dma_start(
-                    out=x_h[:, first : first + PAIR, :],
-                    in_=x_rows[:, first : first + PAIR, h * HD : (h + 1) * HD],
-                )
+        def load(x_rows, x_h, h, first=0, end=SLOTS):
+            nc.sync.dma_start(out=x_h[:, first:end, :], in_=x_rows[:, first:end, h * HD : (h + 1) * HD])
+
+        def new_rows():
+            x_h = heads.tile([P, SLOTS, HD], BF16, tag="x", bufs=3 * H)
             return x_h
 
-        def load(h):
-            k_sb[h] = load_in_pairs(k_rows, h)
-            q_sb[h] = load_in_pairs(q_rows, h)
-            v_h = heads.tile([P, SLOTS, HD], BF16)
-            nc.sync.dma_start(out=v_h[:], in_=v_rows[:, :, h * HD : (h + 1) * HD])
-            v_sb[h] = v_h
-
-        def transpose_slots(x_h):
-            banks = []
-            for first in range(0, SLOTS, PAIR):
-                flipped = small_psum.tile([P, PAIR, P], BF16, tag="small")
-                for j in range(PAIR):
-                    nc.tensor.transpose(flipped[:, j, :], x_h[:, first + j, :], identity[:])
-                banks.append(flipped)
-            return banks
-
-        def copy_out(banks):
+        def new_transposed():
             xT_h = heads.tile([P, SLOTS, P], BF16, tag="xT", bufs=2 * H)
-            for i, flipped in enumerate(banks):
-                nc.vector.tensor_copy(out=xT_h[:, i * PAIR : (i + 1) * PAIR, :], in_=flipped[:])
             return xT_h
 
+        def flip(x_h, xT_h, first, end):
+            flipped = small_psum.tile([P, end - first, P], BF16, tag="small")
+            for j in range(first, end):
+                nc.tensor.transpose(flipped[:, j - first, :], x_h[:, j, :], identity[:])
+            nc.vector.tensor_copy(out=xT_h[:, first:end, :], in_=flipped[:])
+
+        def group_v(h):
+            grouped = heads.tile([P, HD, PACK], BF16, align_bytes=64, tag="v_grouped")
+            nc.gpsimd.tensor_copy(out=grouped[:], in_=v_sb[h][:].rearrange("p j d -> p d j"))
+            v_grouped[h] = grouped
+
         def quantise_v(h):
-            grouped = heads.tile([P, HD, PACK], BF16, align_bytes=64)
-            nc.vector.tensor_copy(out=grouped[:], in_=v_sb[h][:].rearrange("p j d -> p d j"))
             codes = heads.tile([P, HD], U32, align_bytes=64)
             planes = heads.tile([P, HD], U8, align_bytes=64)
             nc.vector.quantize_mx(
                 out=codes[:].bitcast(FP8X4),
                 scales=planes[:],
-                in_=grouped[:].rearrange("p d j -> p (d j)"),
+                in_=v_grouped[h][:].rearrange("p d j -> p (d j)"),
             )
             v_codes[h], v_scales[h] = codes, planes
 
         def write_scores(u):
             h, slot = divmod(u, SLOTS)
-            bank = scores_psum.tile([P, PACK, P], F32)
+            bank = scores_psum.tile([P, PACK, P], F32, tag="bank")
             for j in range(PACK):
                 nc.tensor.matmul(
                     out=bank[:, j, :], lhsT=kT[h][:, j, :], rhs=qT[h][:, slot, :], start=True, stop=True
@@ -113,10 +103,14 @@ def tile_pointwisespaggregatedattention_s_kernel(tc, v, k, q, out):
 
         def multiply_by_v(u):
             h, slot = divmod(u, SLOTS)
-            cols = slice(h * HD, (h + 1) * HD)
-            acc = small_psum.tile([P, HD], F32, tag="small")
+            first = slot % PAIR
+            if first == 0 or u == UNITS - 1:
+                acc = small_psum.tile([P, PAIR, HD], F32, tag="small")
+                results[u] = acc
+            else:
+                results[u] = results[u - 1]
             nc.tensor.matmul_mx(
-                out=acc[:],
+                out=results[u][:, first, :],
                 lhsT=p_codes[u][:].bitcast(FP8X4),
                 lhsT_scale=p_scales[u][:],
                 rhs=v_codes[h][:].bitcast(FP8X4),
@@ -124,13 +118,30 @@ def tile_pointwisespaggregatedattention_s_kernel(tc, v, k, q, out):
                 start=True,
                 stop=True,
             )
-            nc.vector.tensor_copy(out=out_sb[:, slot, cols], in_=acc[:])
-            nc.sync.dma_start(out=out_rows[:, slot, cols], in_=out_sb[:, slot, cols])
+
+        def store(u, count):
+            h, slot = divmod(u, SLOTS)
+            rows, cols = slice(slot, slot + count), slice(h * HD, (h + 1) * HD)
+            first = slot % PAIR
+            nc.vector.tensor_copy(out=out_sb[:, rows, cols], in_=results[u][:, first : first + count, :])
+            nc.sync.dma_start(out=out_rows[:, rows, cols], in_=out_sb[:, rows, cols])
 
         ctx.enter_context(tc.manual_schedule())
 
         for h in range(H):
-            load(h)
+            q_sb[h], k_sb[h], v_sb[h] = new_rows(), new_rows(), new_rows()
+        load(q_rows, q_sb[0], 0, 0, 1)
+        load(k_rows, k_sb[0], 0, 0, 2)
+        load(k_rows, k_sb[0], 0, 2, 4)
+        load(q_rows, q_sb[0], 0, 1, 4)
+        load(k_rows, k_sb[1], 1)
+        load(q_rows, q_sb[1], 1)
+        load(v_rows, v_sb[0], 0)
+        load(v_rows, v_sb[1], 1)
+        for h in range(2, H):
+            load(k_rows, k_sb[h], h)
+            load(q_rows, q_sb[h], h)
+            load(v_rows, v_sb[h], h)
 
         identity = consts.tile([P, P], BF16)
         make_identity(nc, identity[:])
@@ -139,26 +150,39 @@ def tile_pointwisespaggregatedattention_s_kernel(tc, v, k, q, out):
         warm = consts.tile([P, 1], F32)
         nc.scalar.activation(out=warm[:], in_=zero[:], func=SILU)
 
-        kT[0] = copy_out(transpose_slots(k_sb[0]))
-        qT[0] = copy_out(transpose_slots(q_sb[0]))
-        for u in range(SCORES_AHEAD):
-            write_scores(u)
-        quantise_v(0)
+        for h in range(H):
+            kT[h], qT[h] = new_transposed(), new_transposed()
+        for h in range(H):
+            group_v(h)
+        flip(q_sb[0], qT[0], 0, 1)
+        flip(k_sb[0], kT[0], 0, 2)
+        flip(k_sb[0], kT[0], 2, 4)
+        flip(q_sb[0], qT[0], 1, 4)
+        write_scores(0)
+        write_scores(1)
+        flip(k_sb[1], kT[1], 0, SLOTS)
+        write_scores(2)
+        flip(q_sb[1], qT[1], 0, SLOTS)
+        write_scores(3)
 
-        for u in range(-SCORES_AHEAD, UNITS + MX_BEHIND):
-            ahead = u + SCORES_AHEAD
-            ahead_h, ahead_slot = divmod(ahead, SLOTS)
+        for u in range(0, UNITS + MX_BEHIND):
+            if 1 <= u and u + SCORES_AHEAD < UNITS:
+                write_scores(u + SCORES_AHEAD)
             h, slot = divmod(u, SLOTS)
-
-            if ahead_h + 1 < H and ahead_slot == 0:
-                kT[ahead_h + 1] = copy_out(transpose_slots(k_sb[ahead_h + 1]))
-            if ahead_h + 1 < H and ahead_slot == 1:
-                qT[ahead_h + 1] = copy_out(transpose_slots(q_sb[ahead_h + 1]))
-            if SCORES_AHEAD <= ahead < UNITS:
-                write_scores(ahead)
-            if 0 <= u - MX_BEHIND:
-                multiply_by_v(u - MX_BEHIND)
-            if 0 <= u < UNITS:
+            if h + 2 < H and slot == 2:
+                flip(k_sb[h + 2], kT[h + 2], 0, SLOTS)
+            if h + 2 < H and slot == 3:
+                flip(q_sb[h + 2], qT[h + 2], 0, SLOTS)
+            done = u - MX_BEHIND
+            if 0 <= done:
+                multiply_by_v(done)
+            if u == UNITS - 1:
+                store(done - 1, PAIR)
+            if u < UNITS:
                 silu_and_quantise(u)
-            if 0 <= h and h + 1 < H and slot == 2:
-                quantise_v(h + 1)
+            if h < H and slot == 0:
+                quantise_v(h)
+            if 0 <= done < UNITS - PAIR - 1 and done % PAIR == 1:
+                store(done - 1, PAIR)
+        store(UNITS - 2, 1)
+        store(UNITS - 1, 1)

@@ -67,7 +67,7 @@ def tile_pointwisespaggregatedattention_s_kernel(tc, v, k, q, out):
 
         def group_v(h):
             grouped = heads.tile([P, HD, PACK], BF16, align_bytes=64, tag="v_grouped")
-            nc.gpsimd.tensor_copy(out=grouped[:], in_=v_sb[h][:].rearrange("p j d -> p d j"))
+            nc.vector.tensor_copy(out=grouped[:], in_=v_sb[h][:].rearrange("p j d -> p d j"))
             v_grouped[h] = grouped
 
         def quantise_v(h):
@@ -134,11 +134,8 @@ def tile_pointwisespaggregatedattention_s_kernel(tc, v, k, q, out):
         load(k_rows, k_sb[0], 0, 0, 2)
         load(k_rows, k_sb[0], 0, 2, 4)
         load(q_rows, q_sb[0], 0, 1, 4)
-        load(k_rows, k_sb[1], 1)
-        load(q_rows, q_sb[1], 1)
         load(v_rows, v_sb[0], 0)
-        load(v_rows, v_sb[1], 1)
-        for h in range(2, H):
+        for h in range(1, H):
             load(k_rows, k_sb[h], h)
             load(q_rows, q_sb[h], h)
             load(v_rows, v_sb[h], h)
@@ -152,14 +149,13 @@ def tile_pointwisespaggregatedattention_s_kernel(tc, v, k, q, out):
 
         for h in range(H):
             kT[h], qT[h] = new_transposed(), new_transposed()
-        for h in range(H):
-            group_v(h)
         flip(q_sb[0], qT[0], 0, 1)
         flip(k_sb[0], kT[0], 0, 2)
         flip(k_sb[0], kT[0], 2, 4)
         flip(q_sb[0], qT[0], 1, 4)
         write_scores(0)
         write_scores(1)
+        group_v(0)
         flip(k_sb[1], kT[1], 0, SLOTS)
         write_scores(2)
         flip(q_sb[1], qT[1], 0, SLOTS)
@@ -180,8 +176,12 @@ def tile_pointwisespaggregatedattention_s_kernel(tc, v, k, q, out):
                 store(done - 1, PAIR)
             if u < UNITS:
                 silu_and_quantise(u)
-            if h < H and slot == 0:
-                quantise_v(h)
+            if u == 0:
+                quantise_v(0)
+            if h + 1 < H and slot == 1:
+                group_v(h + 1)
+            if h + 1 < H and slot == 3:
+                quantise_v(h + 1)
             if 0 <= done < UNITS - PAIR - 1 and done % PAIR == 1:
                 store(done - 1, PAIR)
         store(UNITS - 2, 1)

@@ -19,8 +19,8 @@ SLOTS = S // P
 PAIR = 2
 UNITS = H * SLOTS
 
-SCORES_AHEAD = 3
-MX_BEHIND = 2
+SCORES_AHEAD = 2
+MX_BEHIND = 4
 
 FLOPS = 2 * (2 * H * S * S * HD)
 
@@ -119,11 +119,11 @@ def tile_pointwisespaggregatedattention_s_kernel(tc, v, k, q, out):
                 stop=True,
             )
 
-        def store(u, count):
+        def store(u, count, copy=nc.vector.tensor_copy):
             h, slot = divmod(u, SLOTS)
             rows, cols = slice(slot, slot + count), slice(h * HD, (h + 1) * HD)
             first = slot % PAIR
-            nc.vector.tensor_copy(out=out_sb[:, rows, cols], in_=results[u][:, first : first + count, :])
+            copy(out=out_sb[:, rows, cols], in_=results[u][:, first : first + count, :])
             nc.sync.dma_start(out=out_rows[:, rows, cols], in_=out_sb[:, rows, cols])
 
         ctx.enter_context(tc.manual_schedule())
@@ -134,11 +134,11 @@ def tile_pointwisespaggregatedattention_s_kernel(tc, v, k, q, out):
         load(k_rows, k_sb[0], 0, 0, 2)
         load(k_rows, k_sb[0], 0, 2, 4)
         load(q_rows, q_sb[0], 0, 1, 4)
-        load(v_rows, v_sb[0], 0)
         for h in range(1, H):
             load(k_rows, k_sb[h], h)
             load(q_rows, q_sb[h], h)
-            load(v_rows, v_sb[h], h)
+            load(v_rows, v_sb[h - 1], h - 1)
+        load(v_rows, v_sb[H - 1], H - 1)
 
         identity = consts.tile([P, P], BF16)
         make_identity(nc, identity[:])
@@ -155,34 +155,37 @@ def tile_pointwisespaggregatedattention_s_kernel(tc, v, k, q, out):
         flip(q_sb[0], qT[0], 1, 4)
         write_scores(0)
         write_scores(1)
-        group_v(0)
         flip(k_sb[1], kT[1], 0, SLOTS)
         write_scores(2)
         flip(q_sb[1], qT[1], 0, SLOTS)
         write_scores(3)
 
-        for u in range(0, UNITS + MX_BEHIND):
-            if 1 <= u and u + SCORES_AHEAD < UNITS:
-                write_scores(u + SCORES_AHEAD)
+        group_v(0)
+
+        multiplied = 0
+        for u in range(UNITS):
             h, slot = divmod(u, SLOTS)
+            if SLOTS <= u + SCORES_AHEAD < UNITS:
+                write_scores(u + SCORES_AHEAD)
             if h + 2 < H and slot == 2:
                 flip(k_sb[h + 2], kT[h + 2], 0, SLOTS)
             if h + 2 < H and slot == 3:
                 flip(q_sb[h + 2], qT[h + 2], 0, SLOTS)
-            done = u - MX_BEHIND
-            if 0 <= done:
-                multiply_by_v(done)
-            if u == UNITS - 1:
-                store(done - 1, PAIR)
-            if u < UNITS:
-                silu_and_quantise(u)
-            if u == 0:
-                quantise_v(0)
-            if h + 1 < H and slot == 1:
+            behind = max(2, min(MX_BEHIND, MX_BEHIND + UNITS - 4 - u))
+            ready = multiplied
+            while multiplied <= u - behind:
+                multiply_by_v(multiplied)
+                multiplied += 1
+            silu_and_quantise(u)
+            if slot == 1:
+                quantise_v(h)
+            if h + 1 < H and slot == 2:
                 group_v(h + 1)
-            if h + 1 < H and slot == 3:
-                quantise_v(h + 1)
-            if 0 <= done < UNITS - PAIR - 1 and done % PAIR == 1:
-                store(done - 1, PAIR)
+            for done in range(ready, multiplied):
+                if done % PAIR == 1 and done < UNITS - PAIR - 1:
+                    store(done - 1, PAIR)
+        store(UNITS - 4, PAIR, nc.scalar.copy)
+        multiply_by_v(UNITS - 2)
+        multiply_by_v(UNITS - 1)
         store(UNITS - 2, 1)
-        store(UNITS - 1, 1)
+        store(UNITS - 1, 1, nc.scalar.copy)

@@ -130,10 +130,10 @@ def tile_pointwisespaggregatedattention_s_kernel(tc, v, k, q, out):
 
         for h in range(H):
             q_sb[h], k_sb[h], v_sb[h] = new_rows(), new_rows(), new_rows()
-        load(q_rows, q_sb[0], 0, 0, 1)
+        load(q_rows, q_sb[0], 0, 0, 2)
         load(k_rows, k_sb[0], 0, 0, 2)
         load(k_rows, k_sb[0], 0, 2, 4)
-        load(q_rows, q_sb[0], 0, 1, 4)
+        load(q_rows, q_sb[0], 0, 2, 4)
         for h in range(1, H):
             load(k_rows, k_sb[h], h)
             load(q_rows, q_sb[h], h)
@@ -149,17 +149,16 @@ def tile_pointwisespaggregatedattention_s_kernel(tc, v, k, q, out):
 
         for h in range(H):
             kT[h], qT[h] = new_transposed(), new_transposed()
-        flip(q_sb[0], qT[0], 0, 1)
-        flip(k_sb[0], kT[0], 0, 2)
-        flip(k_sb[0], kT[0], 2, 4)
-        flip(q_sb[0], qT[0], 1, 4)
+        for x_sb, xT, first in ((q_sb, qT, 0), (k_sb, kT, 0), (k_sb, kT, 2), (q_sb, qT, 2)):
+            flip(x_sb[0], xT[0], first, first + 2)
         write_scores(0)
         write_scores(1)
-        flip(k_sb[1], kT[1], 0, SLOTS)
+        flip(k_sb[1], kT[1], 0, 2)
+        flip(k_sb[1], kT[1], 2, 4)
         write_scores(2)
-        flip(q_sb[1], qT[1], 0, SLOTS)
+        flip(q_sb[1], qT[1], 0, 2)
+        flip(q_sb[1], qT[1], 2, 4)
         write_scores(3)
-
         group_v(0)
 
         multiplied = 0
@@ -167,9 +166,9 @@ def tile_pointwisespaggregatedattention_s_kernel(tc, v, k, q, out):
             h, slot = divmod(u, SLOTS)
             if SLOTS <= u + SCORES_AHEAD < UNITS:
                 write_scores(u + SCORES_AHEAD)
-            if h + 2 < H and slot == 2:
+            if h + 2 < H and slot == 1:
                 flip(k_sb[h + 2], kT[h + 2], 0, SLOTS)
-            if h + 2 < H and slot == 3:
+            if h + 2 < H and slot == 2:
                 flip(q_sb[h + 2], qT[h + 2], 0, SLOTS)
             behind = max(2, min(MX_BEHIND, MX_BEHIND + UNITS - 4 - u))
             ready = multiplied
@@ -177,9 +176,11 @@ def tile_pointwisespaggregatedattention_s_kernel(tc, v, k, q, out):
                 multiply_by_v(multiplied)
                 multiplied += 1
             silu_and_quantise(u)
-            if slot == 1:
-                quantise_v(h)
-            if h + 1 < H and slot == 2:
+            if u == 0:
+                quantise_v(0)
+            if h + 1 < H and slot == 3:
+                quantise_v(h + 1)
+            if h + 1 < H and slot == 1:
                 group_v(h + 1)
             for done in range(ready, multiplied):
                 if done % PAIR == 1 and done < UNITS - PAIR - 1:

@@ -22,6 +22,9 @@ UNITS = H * SLOTS
 SCORES_AHEAD = 2
 MX_BEHIND = 4
 
+WARM_PLAIN = 6
+WARM_MX = 2
+
 FLOPS = 2 * (2 * H * S * S * HD)
 
 
@@ -130,15 +133,19 @@ def tile_pointwisespaggregatedattention_s_kernel(tc, v, k, q, out):
 
         for h in range(H):
             q_sb[h], k_sb[h], v_sb[h] = new_rows(), new_rows(), new_rows()
-        load(q_rows, q_sb[0], 0, 0, 2)
+        load(q_rows, q_sb[0], 0, 0, 1)
         load(k_rows, k_sb[0], 0, 0, 2)
         load(k_rows, k_sb[0], 0, 2, 4)
+        load(q_rows, q_sb[0], 0, 1, 2)
         load(q_rows, q_sb[0], 0, 2, 4)
-        for h in range(1, H):
+        load(k_rows, k_sb[1], 1)
+        load(q_rows, q_sb[1], 1)
+        for h in range(2, H):
             load(k_rows, k_sb[h], h)
+            load(v_rows, v_sb[h - 2], h - 2)
             load(q_rows, q_sb[h], h)
-            load(v_rows, v_sb[h - 1], h - 1)
-        load(v_rows, v_sb[H - 1], H - 1)
+        for h in range(H - 2, H):
+            load(v_rows, v_sb[h], h)
 
         identity = consts.tile([P, P], BF16)
         make_identity(nc, identity[:])
@@ -147,10 +154,35 @@ def tile_pointwisespaggregatedattention_s_kernel(tc, v, k, q, out):
         warm = consts.tile([P, 1], F32)
         nc.scalar.activation(out=warm[:], in_=zero[:], func=SILU)
 
+        zeros = consts.tile([P, P * PACK], BF16, align_bytes=64)
+        nc.vector.memset(zeros[:, :P], 0.0)
+        nc.vector.memset(zeros[:, P:], 0.0)
+        zero_codes = consts.tile([P, P], U32, align_bytes=64)
+        zero_planes = consts.tile([P, P], U8, align_bytes=64)
+        nc.vector.quantize_mx(out=zero_codes[:].bitcast(FP8X4), scales=zero_planes[:], in_=zeros[:])
+        unread = scores_psum.tile([P, PACK, P], F32, tag="bank")
+        for i in range(WARM_PLAIN):
+            nc.tensor.matmul(
+                out=unread[:, i % PACK, :], lhsT=zeros[:, :P], rhs=zeros[:, :P], start=True, stop=True
+            )
+        for i in range(WARM_MX):
+            nc.tensor.matmul_mx(
+                out=unread[:, i % PACK, :],
+                lhsT=zero_codes[:].bitcast(FP8X4),
+                lhsT_scale=zero_planes[:],
+                rhs=zero_codes[:].bitcast(FP8X4),
+                rhs_scale=zero_planes[:],
+                start=True,
+                stop=True,
+            )
+
         for h in range(H):
             kT[h], qT[h] = new_transposed(), new_transposed()
-        for x_sb, xT, first in ((q_sb, qT, 0), (k_sb, kT, 0), (k_sb, kT, 2), (q_sb, qT, 2)):
-            flip(x_sb[0], xT[0], first, first + 2)
+        flip(q_sb[0], qT[0], 0, 1)
+        flip(k_sb[0], kT[0], 0, 2)
+        flip(k_sb[0], kT[0], 2, 4)
+        flip(q_sb[0], qT[0], 1, 2)
+        flip(q_sb[0], qT[0], 2, 4)
         write_scores(0)
         write_scores(1)
         flip(k_sb[1], kT[1], 0, 2)
@@ -159,7 +191,6 @@ def tile_pointwisespaggregatedattention_s_kernel(tc, v, k, q, out):
         flip(q_sb[1], qT[1], 0, 2)
         flip(q_sb[1], qT[1], 2, 4)
         write_scores(3)
-        group_v(0)
 
         multiplied = 0
         for u in range(UNITS):
@@ -168,7 +199,7 @@ def tile_pointwisespaggregatedattention_s_kernel(tc, v, k, q, out):
                 write_scores(u + SCORES_AHEAD)
             if h + 2 < H and slot == 1:
                 flip(k_sb[h + 2], kT[h + 2], 0, SLOTS)
-            if h + 2 < H and slot == 2:
+            if h + 2 < H and slot == 3:
                 flip(q_sb[h + 2], qT[h + 2], 0, SLOTS)
             behind = max(2, min(MX_BEHIND, MX_BEHIND + UNITS - 4 - u))
             ready = multiplied
@@ -176,12 +207,10 @@ def tile_pointwisespaggregatedattention_s_kernel(tc, v, k, q, out):
                 multiply_by_v(multiplied)
                 multiplied += 1
             silu_and_quantise(u)
-            if u == 0:
-                quantise_v(0)
-            if h + 1 < H and slot == 3:
-                quantise_v(h + 1)
-            if h + 1 < H and slot == 1:
-                group_v(h + 1)
+            if slot == 0:
+                group_v(h)
+            if slot == 1:
+                quantise_v(h)
             for done in range(ready, multiplied):
                 if done % PAIR == 1 and done < UNITS - PAIR - 1:
                     store(done - 1, PAIR)

@@ -85,16 +85,24 @@ def tile_pointwisespaggregatedattention_s_kernel(tc, v, k, q, out):
 
         def write_scores(u):
             h, slot = divmod(u, SLOTS)
-            bank = scores_psum.tile([P, PACK, P], F32, tag="bank")
+            bank = scores_psum.tile([P, P // 2, PACK, 2], F32, tag="bank")
             for j in range(PACK):
                 nc.tensor.matmul(
-                    out=bank[:, j, :], lhsT=kT[h][:, j, :], rhs=qT[h][:, slot, :], start=True, stop=True
+                    out=bank[:, :, j, :],
+                    lhsT=kT[h][:, j, :],
+                    rhs=qT[h][:, slot, :].rearrange("p (n i) -> p n i", i=2),
+                    start=True,
+                    stop=True,
                 )
             scores[u] = bank
 
         def silu_and_quantise(u):
             grouped = units.tile([P, P, PACK], BF16, align_bytes=64)
-            nc.scalar.activation(out=grouped[:], in_=scores[u][:].rearrange("p j n -> p n j"), func=SILU)
+            nc.scalar.activation(
+                out=grouped[:].rearrange("p (n i) j -> p n i j", i=2),
+                in_=scores[u][:].rearrange("p n j i -> p n i j"),
+                func=SILU,
+            )
             codes = units.tile([P, P], U32, align_bytes=64)
             planes = units.tile([P, P], U8, align_bytes=64)
             nc.vector.quantize_mx(

@@ -40,14 +40,15 @@ def tile_pointwisespaggregatedattention_s_kernel(tc, v, k, q, out):
     with ExitStack() as ctx:
         consts = ctx.enter_context(tc.tile_pool(name="consts", bufs=1))
         heads = ctx.enter_context(tc.tile_pool(name="heads", bufs=H))
-        units = ctx.enter_context(tc.tile_pool(name="units", bufs=SCORES_AHEAD + MX_BEHIND + 1))
+        pairs = ctx.enter_context(tc.tile_pool(name="pairs", bufs=UNITS // PAIR))
         scores_psum = ctx.enter_context(tc.psum_pool(name="scores_psum", bufs=4))
         small_psum = ctx.enter_context(tc.psum_pool(name="small_psum", bufs=4))
 
         k_sb, q_sb, v_sb = {}, {}, {}
         kT, qT = {}, {}
         v_grouped, v_codes, v_scales = {}, {}, {}
-        scores, p_codes, p_scales = {}, {}, {}
+        scores = {}
+        p_grouped, p_codes, p_scales = {}, {}, {}
         results = {}
         out_sb = consts.tile([P, SLOTS, H * HD], F32)
 
@@ -96,45 +97,48 @@ def tile_pointwisespaggregatedattention_s_kernel(tc, v, k, q, out):
                 )
             scores[u] = bank
 
-        def silu_and_quantise(u):
-            grouped = units.tile([P, P, PACK], BF16, align_bytes=64)
+        def silu(u):
+            i, half = divmod(u, PAIR)
+            if half == 0:
+                grouped = pairs.tile([P, PAIR, P, PACK], BF16, align_bytes=64, tag="grouped")
+                codes = pairs.tile([P, PAIR, P], U32, align_bytes=64, tag="codes")
+                planes = pairs.tile([P, PAIR, P], U8, align_bytes=64, tag="planes")
+                p_grouped[i], p_codes[i], p_scales[i] = grouped, codes, planes
             nc.scalar.activation(
-                out=grouped[:].rearrange("p (n i) j -> p n i j", i=2),
+                out=p_grouped[i][:, half].rearrange("p (n i) j -> p n i j", i=2),
                 in_=scores[u][:].rearrange("p n j i -> p n i j"),
                 func=SILU,
             )
-            codes = units.tile([P, P], U32, align_bytes=64)
-            planes = units.tile([P, P], U8, align_bytes=64)
-            nc.vector.quantize_mx(
-                out=codes[:].bitcast(FP8X4),
-                scales=planes[:],
-                in_=grouped[:].rearrange("p n j -> p (n j)"),
-            )
-            p_codes[u], p_scales[u] = codes, planes
 
-        def multiply_by_v(u):
-            h, slot = divmod(u, SLOTS)
-            first = slot % PAIR
-            if first == 0 or u == UNITS - 1:
-                acc = small_psum.tile([P, PAIR, HD], F32, tag="small")
-                results[u] = acc
-            else:
-                results[u] = results[u - 1]
-            nc.tensor.matmul_mx(
-                out=results[u][:, first, :],
-                lhsT=p_codes[u][:].bitcast(FP8X4),
-                lhsT_scale=p_scales[u][:],
-                rhs=v_codes[h][:].bitcast(FP8X4),
-                rhs_scale=v_scales[h][:],
-                start=True,
-                stop=True,
+        def quantise(u, count=PAIR):
+            i, half = divmod(u, PAIR)
+            units_of = slice(half, half + count)
+            nc.vector.quantize_mx(
+                out=p_codes[i][:, units_of].rearrange("p u n -> p (u n)").bitcast(FP8X4),
+                scales=p_scales[i][:, units_of].rearrange("p u n -> p (u n)"),
+                in_=p_grouped[i][:, units_of].rearrange("p u n j -> p (u n j)"),
             )
+
+        def multiply_by_v(u, count):
+            h, slot = divmod(u, SLOTS)
+            acc = small_psum.tile([P, count, HD], F32, tag="small")
+            for n in range(count):
+                i, half = divmod(u + n, PAIR)
+                nc.tensor.matmul_mx(
+                    out=acc[:, n, :],
+                    lhsT=p_codes[i][:, half].bitcast(FP8X4),
+                    lhsT_scale=p_scales[i][:, half],
+                    rhs=v_codes[h][:].bitcast(FP8X4),
+                    rhs_scale=v_scales[h][:],
+                    start=True,
+                    stop=True,
+                )
+            results[u] = acc
 
         def store(u, count, copy=nc.vector.tensor_copy):
             h, slot = divmod(u, SLOTS)
             rows, cols = slice(slot, slot + count), slice(h * HD, (h + 1) * HD)
-            first = slot % PAIR
-            copy(out=out_sb[:, rows, cols], in_=results[u][:, first : first + count, :])
+            copy(out=out_sb[:, rows, cols], in_=results[u][:])
             nc.sync.dma_start(out=out_rows[:, rows, cols], in_=out_sb[:, rows, cols])
 
         ctx.enter_context(tc.manual_schedule())
@@ -200,30 +204,41 @@ def tile_pointwisespaggregatedattention_s_kernel(tc, v, k, q, out):
         flip(q_sb[1], qT[1], 2, 4)
         write_scores(3)
 
-        multiplied = 0
-        for u in range(UNITS):
-            h, slot = divmod(u, SLOTS)
-            if SLOTS <= u + SCORES_AHEAD < UNITS:
-                write_scores(u + SCORES_AHEAD)
-            if h + 2 < H and slot == 1:
-                flip(k_sb[h + 2], kT[h + 2], 0, SLOTS)
-            if h + 2 < H and slot == 3:
-                flip(q_sb[h + 2], qT[h + 2], 0, SLOTS)
-            behind = max(2, min(MX_BEHIND, MX_BEHIND + UNITS - 4 - u))
-            ready = multiplied
-            while multiplied <= u - behind:
-                multiply_by_v(multiplied)
-                multiplied += 1
-            silu_and_quantise(u)
-            if slot == 0:
-                group_v(h)
-            if slot == 1:
-                quantise_v(h)
-            for done in range(ready, multiplied):
-                if done % PAIR == 1 and done < UNITS - PAIR - 1:
-                    store(done - 1, PAIR)
-        store(UNITS - 4, PAIR, nc.scalar.copy)
-        multiply_by_v(UNITS - 2)
-        multiply_by_v(UNITS - 1)
-        store(UNITS - 2, 1)
-        store(UNITS - 1, 1, nc.scalar.copy)
+        for i in range(UNITS // PAIR):
+            u = PAIR * i
+            if i >= 1 and u + 2 < UNITS:
+                write_scores(u + 2)
+            if i >= 1 and i<7:
+                quantise(u - PAIR)
+            if i < 4:
+                h = 2 + i // 2
+                if i % 2 == 0:
+                    flip(k_sb[h], kT[h], 0, SLOTS)
+                else:
+                    flip(q_sb[h], qT[h], 0, SLOTS)
+            silu(u)
+            if i >= 1 and u + 3 < UNITS:
+                write_scores(u + 3)
+            silu(u + 1)
+            if i in (1, 2, 4, 5):
+                group_v((1, 2, 4, 5).index(i))
+            if i in (2, 3, 5, 6):
+                quantise_v((2, 3, 5, 6).index(i))
+            if i in (3, 5):
+                multiply_by_v(2 * (i - 3), SLOTS)
+                store(2 * (i - 3), SLOTS)
+            if i == 6:
+                multiply_by_v(8, 2)
+                quantise(u)
+                store(8, 2)
+                multiply_by_v(10, 2)
+            if i == 7:
+                store(10, 2)
+                quantise(u, 1)
+                multiply_by_v(12, 2)
+                quantise(u + 1, 1)
+        multiply_by_v(14, 1)
+        store(12, 2, nc.scalar.copy)
+        multiply_by_v(15, 1)
+        store(14, 1)
+        store(15, 1, nc.scalar.copy)

@@ -71,7 +71,10 @@ def tile_pointwisespaggregatedattention_s_kernel(tc, v, k, q, out):
 
         def group_v(h):
             grouped = heads.tile([P, HD, PACK], BF16, align_bytes=64, tag="v_grouped")
-            nc.vector.tensor_copy(out=grouped[:], in_=v_sb[h][:].rearrange("p j d -> p d j"))
+            nc.vector.tensor_copy(
+                out=grouped[:].rearrange("p (n i) j -> p n j i", i=4),
+                in_=v_sb[h][:].rearrange("p j (n i) -> p n j i", i=4),
+            )
             v_grouped[h] = grouped
 
         def quantise_v(h):

@@ -8,6 +8,7 @@ F32 = mybir.dt.float32
 U32 = mybir.dt.uint32
 U8 = mybir.dt.uint8
 FP8X4 = mybir.dt.float8_e4m3fn_x4
+MULT, ADD = mybir.AluOpType.mult, mybir.AluOpType.add
 SILU = mybir.ActivationFunctionType.Silu
 
 P = 128
@@ -48,6 +49,7 @@ def tile_pointwisespaggregatedattention_s_kernel(tc, v, k, q, out):
         kT, qT = {}, {}
         v_grouped, v_codes, v_scales = {}, {}, {}
         scores = {}
+        first_rows = consts.tile([P, PACK, P], BF16)
         p_grouped, p_codes, p_scales = {}, {}, {}
         results = {}
         out_sb = consts.tile([P, SLOTS, H * HD], F32)
@@ -87,6 +89,18 @@ def tile_pointwisespaggregatedattention_s_kernel(tc, v, k, q, out):
             )
             v_codes[h], v_scales[h] = codes, planes
 
+        def write_half(first):
+            half = scores_psum.tile([P, PAIR, P], F32, tag="bank")
+            for j in range(PAIR):
+                nc.tensor.matmul(
+                    out=half[:, j, :],
+                    lhsT=kT[0][:, first + j, :],
+                    rhs=qT[0][:, 0, :],
+                    start=True,
+                    stop=True,
+                )
+            nc.scalar.activation(out=first_rows[:, first : first + PAIR, :], in_=half[:], func=SILU)
+
         def write_scores(u):
             h, slot = divmod(u, SLOTS)
             bank = scores_psum.tile([P, P // 2, PACK, 2], F32, tag="bank")
@@ -100,13 +114,24 @@ def tile_pointwisespaggregatedattention_s_kernel(tc, v, k, q, out):
                 )
             scores[u] = bank
 
+        def new_pair(i):
+            grouped = pairs.tile([P, PAIR, P, PACK], BF16, align_bytes=64, tag="grouped")
+            codes = pairs.tile([P, PAIR, P], U32, align_bytes=64, tag="codes")
+            planes = pairs.tile([P, PAIR, P], U8, align_bytes=64, tag="planes")
+            p_grouped[i], p_codes[i], p_scales[i] = grouped, codes, planes
+
+        def group_first():
+            nc.gpsimd.tensor_scalar(
+                out=p_grouped[0][:, 0],
+                in0=first_rows[:].rearrange("p j n -> p n j"),
+                scalar1=1.0,
+                scalar2=0.0,
+                op0=MULT,
+                op1=ADD,
+            )
+
         def silu(u):
             i, half = divmod(u, PAIR)
-            if half == 0:
-                grouped = pairs.tile([P, PAIR, P, PACK], BF16, align_bytes=64, tag="grouped")
-                codes = pairs.tile([P, PAIR, P], U32, align_bytes=64, tag="codes")
-                planes = pairs.tile([P, PAIR, P], U8, align_bytes=64, tag="planes")
-                p_grouped[i], p_codes[i], p_scales[i] = grouped, codes, planes
             nc.scalar.activation(
                 out=p_grouped[i][:, half].rearrange("p (n i) j -> p n i j", i=2),
                 in_=scores[u][:].rearrange("p n j i -> p n i j"),
@@ -146,21 +171,30 @@ def tile_pointwisespaggregatedattention_s_kernel(tc, v, k, q, out):
 
         ctx.enter_context(tc.manual_schedule())
 
-        for h in range(H):
-            q_sb[h], k_sb[h], v_sb[h] = new_rows(), new_rows(), new_rows()
+        def load_heads(x_rows, x_sb, first, count):
+            rows = heads.tile([P, SLOTS, count * HD], BF16, tag="rows%d" % count, bufs=3 * H)
+            cols = slice(first * HD, (first + count) * HD)
+            nc.sync.dma_start(out=rows[:], in_=x_rows[:, :, cols])
+            for n in range(count):
+                x_sb[first + n] = rows[:, :, n * HD : (n + 1) * HD]
+
+        for h in range(1):
+            q_sb[h], k_sb[h] = new_rows(), new_rows()
         load(q_rows, q_sb[0], 0, 0, 1)
         load(k_rows, k_sb[0], 0, 0, 2)
         load(k_rows, k_sb[0], 0, 2, 4)
         load(q_rows, q_sb[0], 0, 1, 2)
         load(q_rows, q_sb[0], 0, 2, 4)
-        load(k_rows, k_sb[1], 1)
-        load(q_rows, q_sb[1], 1)
-        for h in range(2, H):
-            load(k_rows, k_sb[h], h)
-            load(v_rows, v_sb[h - 2], h - 2)
-            load(q_rows, q_sb[h], h)
-        for h in range(H - 2, H):
-            load(v_rows, v_sb[h], h)
+        load_heads(k_rows, k_sb, 1, 1)
+        load_heads(q_rows, q_sb, 1, 1)
+        load_heads(k_rows, k_sb, 2, 1)
+        load_heads(q_rows, q_sb, 2, 1)
+        load_heads(v_rows, v_sb, 0, 1)
+        load_heads(k_rows, k_sb, 3, 1)
+        load_heads(v_rows, v_sb, 1, 1)
+        load_heads(q_rows, q_sb, 3, 1)
+        load_heads(v_rows, v_sb, 2, 1)
+        load_heads(v_rows, v_sb, 3, 1)
 
         identity = consts.tile([P, P], BF16)
         make_identity(nc, identity[:])
@@ -196,9 +230,13 @@ def tile_pointwisespaggregatedattention_s_kernel(tc, v, k, q, out):
         flip(q_sb[0], qT[0], 0, 1)
         flip(k_sb[0], kT[0], 0, 2)
         flip(k_sb[0], kT[0], 2, 4)
+        for i in range(UNITS // PAIR):
+            new_pair(i)
         flip(q_sb[0], qT[0], 1, 2)
+        write_half(0)
         flip(q_sb[0], qT[0], 2, 4)
-        write_scores(0)
+        write_half(PAIR)
+        group_first()
         write_scores(1)
         flip(k_sb[1], kT[1], 0, 2)
         flip(k_sb[1], kT[1], 2, 4)
@@ -207,39 +245,63 @@ def tile_pointwisespaggregatedattention_s_kernel(tc, v, k, q, out):
         flip(q_sb[1], qT[1], 2, 4)
         write_scores(3)
 
-        for i in range(UNITS // PAIR):
-            u = PAIR * i
-            if i >= 1 and u + 2 < UNITS:
-                write_scores(u + 2)
-            if i >= 1 and i<7:
-                quantise(u - PAIR)
-            if i < 4:
-                h = 2 + i // 2
-                if i % 2 == 0:
-                    flip(k_sb[h], kT[h], 0, SLOTS)
-                else:
-                    flip(q_sb[h], qT[h], 0, SLOTS)
-            silu(u)
-            if i >= 1 and u + 3 < UNITS:
-                write_scores(u + 3)
-            silu(u + 1)
-            if i in (1, 2, 4, 5):
-                group_v((1, 2, 4, 5).index(i))
-            if i in (2, 3, 5, 6):
-                quantise_v((2, 3, 5, 6).index(i))
-            if i in (3, 5):
-                multiply_by_v(2 * (i - 3), SLOTS)
-                store(2 * (i - 3), SLOTS)
-            if i == 6:
-                multiply_by_v(8, 2)
-                quantise(u)
-                store(8, 2)
-                multiply_by_v(10, 2)
-            if i == 7:
-                store(10, 2)
-                quantise(u, 1)
-                multiply_by_v(12, 2)
-                quantise(u + 1, 1)
+        flip(k_sb[2], kT[2], 0, SLOTS)
+        silu(1)
+        write_scores(4)
+        quantise(0)
+        flip(q_sb[2], qT[2], 0, SLOTS)
+        silu(2)
+        write_scores(5)
+        silu(3)
+        group_v(0)
+        write_scores(6)
+        quantise(2)
+        silu(4)
+        write_scores(7)
+        silu(5)
+        group_v(1)
+        quantise_v(0)
+        write_scores(8)
+        quantise(4)
+        flip(k_sb[3], kT[3], 0, SLOTS)
+        silu(6)
+        write_scores(9)
+        silu(7)
+        flip(q_sb[3], qT[3], 0, SLOTS)
+        quantise_v(1)
+        multiply_by_v(0, 4)
+        store(0, 4)
+        write_scores(10)
+        quantise(6)
+        silu(8)
+        write_scores(11)
+        silu(9)
+        group_v(2)
+        write_scores(12)
+        quantise(8)
+        silu(10)
+        write_scores(13)
+        silu(11)
+        group_v(3)
+        quantise_v(2)
+        multiply_by_v(4, 4)
+        store(4, 4)
+        write_scores(14)
+        quantise(10)
+        silu(12)
+        write_scores(15)
+        silu(13)
+        quantise_v(3)
+        multiply_by_v(8, 2)
+        quantise(12)
+        store(8, 2)
+        multiply_by_v(10, 2)
+        silu(14)
+        silu(15)
+        store(10, 2)
+        quantise(14, 1)
+        multiply_by_v(12, 2)
+        quantise(15, 1)
         multiply_by_v(14, 1)
         store(12, 2, nc.scalar.copy)
         multiply_by_v(15, 1)

@@ -121,14 +121,7 @@ def tile_pointwisespaggregatedattention_s_kernel(tc, v, k, q, out):
             p_grouped[i], p_codes[i], p_scales[i] = grouped, codes, planes
 
         def group_first():
-            nc.gpsimd.tensor_scalar(
-                out=p_grouped[0][:, 0],
-                in0=first_rows[:].rearrange("p j n -> p n j"),
-                scalar1=1.0,
-                scalar2=0.0,
-                op0=MULT,
-                op1=ADD,
-            )
+            nc.vector.tensor_copy(out=p_grouped[0][:, 0], in_=first_rows[:].rearrange("p j n -> p n j"))
 
         def silu(u):
             i, half = divmod(u, PAIR)
@@ -236,13 +229,13 @@ def tile_pointwisespaggregatedattention_s_kernel(tc, v, k, q, out):
         write_half(0)
         flip(q_sb[0], qT[0], 2, 4)
         write_half(PAIR)
-        group_first()
         write_scores(1)
         flip(k_sb[1], kT[1], 0, 2)
         flip(k_sb[1], kT[1], 2, 4)
         write_scores(2)
         flip(q_sb[1], qT[1], 0, 2)
         flip(q_sb[1], qT[1], 2, 4)
+        group_first()
         write_scores(3)
 
         flip(k_sb[2], kT[2], 0, SLOTS)

from contextlib import ExitStack

import concourse.mybir as mybir
from concourse.masks import make_identity

BF16 = mybir.dt.bfloat16
F32 = mybir.dt.float32
U32 = mybir.dt.uint32
U8 = mybir.dt.uint8
FP8X4 = mybir.dt.float8_e4m3fn_x4
MULT, ADD = mybir.AluOpType.mult, mybir.AluOpType.add
SILU = mybir.ActivationFunctionType.Silu

P = 128
PACK = 4
S = 512
H = 4
HD = 128
SLOTS = S // P
PAIR = 2
UNITS = H * SLOTS

SCORES_AHEAD = 2
MX_BEHIND = 4

WARM_PLAIN = 6
WARM_MX = 2

FLOPS = 2 * (2 * H * S * S * HD)


def tile_pointwisespaggregatedattention_s_kernel(tc, v, k, q, out):
    nc = tc.nc
    assert SLOTS == PACK

    def by_partition(x):
        return x.flatten_outer_dims().rearrange("(p j) d -> p j d", j=SLOTS)

    v_rows, k_rows, q_rows, out_rows = by_partition(v), by_partition(k), by_partition(q), by_partition(out)

    with ExitStack() as ctx:
        consts = ctx.enter_context(tc.tile_pool(name="consts", bufs=1))
        heads = ctx.enter_context(tc.tile_pool(name="heads", bufs=H))
        pairs = ctx.enter_context(tc.tile_pool(name="pairs", bufs=UNITS // PAIR))
        scores_psum = ctx.enter_context(tc.psum_pool(name="scores_psum", bufs=4))
        small_psum = ctx.enter_context(tc.psum_pool(name="small_psum", bufs=4))

        k_sb, q_sb, v_sb = {}, {}, {}
        kT, qT = {}, {}
        v_grouped, v_codes, v_scales = {}, {}, {}
        scores = {}
        first_rows = consts.tile([P, PACK, P], BF16)
        p_grouped, p_codes, p_scales = {}, {}, {}
        results = {}
        out_sb = consts.tile([P, SLOTS, H * HD], F32)

        def load(x_rows, x_h, h, first=0, end=SLOTS):
            nc.sync.dma_start(out=x_h[:, first:end, :], in_=x_rows[:, first:end, h * HD : (h + 1) * HD])

        def new_rows():
            x_h = heads.tile([P, SLOTS, HD], BF16, tag="x", bufs=3 * H)
            return x_h

        def new_transposed():
            xT_h = heads.tile([P, SLOTS, P], BF16, tag="xT", bufs=2 * H)
            return xT_h

        def flip(x_h, xT_h, first, end):
            flipped = small_psum.tile([P, end - first, P], BF16, tag="small")
            for j in range(first, end):
                nc.tensor.transpose(flipped[:, j - first, :], x_h[:, j, :], identity[:])
            nc.vector.tensor_copy(out=xT_h[:, first:end, :], in_=flipped[:])

        def group_v(h):
            grouped = heads.tile([P, HD, PACK], BF16, align_bytes=64, tag="v_grouped")
            nc.vector.tensor_copy(
                out=grouped[:].rearrange("p (n i) j -> p n j i", i=4),
                in_=v_sb[h][:].rearrange("p j (n i) -> p n j i", i=4),
            )
            v_grouped[h] = grouped

        def quantise_v(h):
            codes = heads.tile([P, HD], U32, align_bytes=64)
            planes = heads.tile([P, HD], U8, align_bytes=64)
            nc.vector.quantize_mx(
                out=codes[:].bitcast(FP8X4),
                scales=planes[:],
                in_=v_grouped[h][:].rearrange("p d j -> p (d j)"),
            )
            v_codes[h], v_scales[h] = codes, planes

        def write_half(first):
            half = scores_psum.tile([P, PAIR, P], F32, tag="bank")
            for j in range(PAIR):
                nc.tensor.matmul(
                    out=half[:, j, :],
                    lhsT=kT[0][:, first + j, :],
                    rhs=qT[0][:, 0, :],
                    start=True,
                    stop=True,
                )
            nc.scalar.activation(out=first_rows[:, first : first + PAIR, :], in_=half[:], func=SILU)

        def write_scores(u):
            h, slot = divmod(u, SLOTS)
            bank = scores_psum.tile([P, P // 2, PACK, 2], F32, tag="bank")
            for j in range(PACK):
                nc.tensor.matmul(
                    out=bank[:, :, j, :],
                    lhsT=kT[h][:, j, :],
                    rhs=qT[h][:, slot, :].rearrange("p (n i) -> p n i", i=2),
                    start=True,
                    stop=True,
                )
            scores[u] = bank

        def new_pair(i):
            grouped = pairs.tile([P, PAIR, P, PACK], BF16, align_bytes=64, tag="grouped")
            codes = pairs.tile([P, PAIR, P], U32, align_bytes=64, tag="codes")
            planes = pairs.tile([P, PAIR, P], U8, align_bytes=64, tag="planes")
            p_grouped[i], p_codes[i], p_scales[i] = grouped, codes, planes

        def group_first():
            nc.vector.tensor_copy(out=p_grouped[0][:, 0], in_=first_rows[:].rearrange("p j n -> p n j"))

        def silu(u):
            i, half = divmod(u, PAIR)
            nc.scalar.activation(
                out=p_grouped[i][:, half].rearrange("p (n i) j -> p n i j", i=2),
                in_=scores[u][:].rearrange("p n j i -> p n i j"),
                func=SILU,
            )

        def quantise(u, count=PAIR):
            i, half = divmod(u, PAIR)
            units_of = slice(half, half + count)
            nc.vector.quantize_mx(
                out=p_codes[i][:, units_of].rearrange("p u n -> p (u n)").bitcast(FP8X4),
                scales=p_scales[i][:, units_of].rearrange("p u n -> p (u n)"),
                in_=p_grouped[i][:, units_of].rearrange("p u n j -> p (u n j)"),
            )

        def multiply_by_v(u, count):
            h, slot = divmod(u, SLOTS)
            acc = small_psum.tile([P, count, HD], F32, tag="small")
            for n in range(count):
                i, half = divmod(u + n, PAIR)
                nc.tensor.matmul_mx(
                    out=acc[:, n, :],
                    lhsT=p_codes[i][:, half].bitcast(FP8X4),
                    lhsT_scale=p_scales[i][:, half],
                    rhs=v_codes[h][:].bitcast(FP8X4),
                    rhs_scale=v_scales[h][:],
                    start=True,
                    stop=True,
                )
            results[u] = acc

        def store(u, count, copy=nc.vector.tensor_copy):
            h, slot = divmod(u, SLOTS)
            rows, cols = slice(slot, slot + count), slice(h * HD, (h + 1) * HD)
            copy(out=out_sb[:, rows, cols], in_=results[u][:])
            nc.sync.dma_start(out=out_rows[:, rows, cols], in_=out_sb[:, rows, cols])

        ctx.enter_context(tc.manual_schedule())

        def load_heads(x_rows, x_sb, first, count):
            rows = heads.tile([P, SLOTS, count * HD], BF16, tag="rows%d" % count, bufs=3 * H)
            cols = slice(first * HD, (first + count) * HD)
            nc.sync.dma_start(out=rows[:], in_=x_rows[:, :, cols])
            for n in range(count):
                x_sb[first + n] = rows[:, :, n * HD : (n + 1) * HD]

        for h in range(1):
            q_sb[h], k_sb[h] = new_rows(), new_rows()
        load(q_rows, q_sb[0], 0, 0, 1)
        load(k_rows, k_sb[0], 0, 0, 2)
        load(k_rows, k_sb[0], 0, 2, 4)
        load(q_rows, q_sb[0], 0, 1, 2)
        load(q_rows, q_sb[0], 0, 2, 4)
        load_heads(k_rows, k_sb, 1, 1)
        load_heads(q_rows, q_sb, 1, 1)
        load_heads(k_rows, k_sb, 2, 1)
        load_heads(q_rows, q_sb, 2, 1)
        load_heads(v_rows, v_sb, 0, 1)
        load_heads(k_rows, k_sb, 3, 1)
        load_heads(v_rows, v_sb, 1, 1)
        load_heads(q_rows, q_sb, 3, 1)
        load_heads(v_rows, v_sb, 2, 1)
        load_heads(v_rows, v_sb, 3, 1)

        identity = consts.tile([P, P], BF16)
        make_identity(nc, identity[:])
        zero = consts.tile([P, 1], F32)
        nc.vector.memset(zero[:], 0.0)
        warm = consts.tile([P, 1], F32)
        nc.scalar.activation(out=warm[:], in_=zero[:], func=SILU)

        zeros = consts.tile([P, P * PACK], BF16, align_bytes=64)
        nc.vector.memset(zeros[:, :P], 0.0)
        nc.vector.memset(zeros[:, P:], 0.0)
        zero_codes = consts.tile([P, P], U32, align_bytes=64)
        zero_planes = consts.tile([P, P], U8, align_bytes=64)
        nc.vector.quantize_mx(out=zero_codes[:].bitcast(FP8X4), scales=zero_planes[:], in_=zeros[:])
        unread = scores_psum.tile([P, PACK, P], F32, tag="bank")
        for i in range(WARM_PLAIN):
            nc.tensor.matmul(
                out=unread[:, i % PACK, :], lhsT=zeros[:, :P], rhs=zeros[:, :P], start=True, stop=True
            )
        for i in range(WARM_MX):
            nc.tensor.matmul_mx(
                out=unread[:, i % PACK, :],
                lhsT=zero_codes[:].bitcast(FP8X4),
                lhsT_scale=zero_planes[:],
                rhs=zero_codes[:].bitcast(FP8X4),
                rhs_scale=zero_planes[:],
                start=True,
                stop=True,
            )

        for h in range(H):
            kT[h], qT[h] = new_transposed(), new_transposed()
        flip(q_sb[0], qT[0], 0, 1)
        flip(k_sb[0], kT[0], 0, 2)
        flip(k_sb[0], kT[0], 2, 4)
        for i in range(UNITS // PAIR):
            new_pair(i)
        flip(q_sb[0], qT[0], 1, 2)
        write_half(0)
        flip(q_sb[0], qT[0], 2, 4)
        write_half(PAIR)
        write_scores(1)
        flip(k_sb[1], kT[1], 0, 2)
        flip(k_sb[1], kT[1], 2, 4)
        write_scores(2)
        flip(q_sb[1], qT[1], 0, 2)
        flip(q_sb[1], qT[1], 2, 4)
        group_first()
        write_scores(3)

        flip(k_sb[2], kT[2], 0, SLOTS)
        silu(1)
        write_scores(4)
        quantise(0)
        flip(q_sb[2], qT[2], 0, SLOTS)
        silu(2)
        write_scores(5)
        silu(3)
        group_v(0)
        write_scores(6)
        quantise(2)
        silu(4)
        write_scores(7)
        silu(5)
        group_v(1)
        quantise_v(0)
        write_scores(8)
        quantise(4)
        flip(k_sb[3], kT[3], 0, SLOTS)
        silu(6)
        write_scores(9)
        silu(7)
        flip(q_sb[3], qT[3], 0, SLOTS)
        quantise_v(1)
        multiply_by_v(0, 4)
        store(0, 4)
        write_scores(10)
        quantise(6)
        silu(8)
        write_scores(11)
        silu(9)
        group_v(2)
        write_scores(12)
        quantise(8)
        silu(10)
        write_scores(13)
        silu(11)
        group_v(3)
        quantise_v(2)
        multiply_by_v(4, 4)
        store(4, 4)
        write_scores(14)
        quantise(10)
        silu(12)
        write_scores(15)
        silu(13)
        quantise_v(3)
        multiply_by_v(8, 2)
        quantise(12)
        store(8, 2)
        multiply_by_v(10, 2)
        silu(14)
        silu(15)
        store(10, 2)
        quantise(14, 1)
        multiply_by_v(12, 2)
        quantise(15, 1)
        multiply_by_v(14, 1)
        store(12, 2, nc.scalar.copy)
        multiply_by_v(15, 1)
        store(14, 1)
        store(15, 1, nc.scalar.copy)
